import numpy as np
import ml_dtypes


def mxq(x, axis, fmt="e4m3"):
    dtype, down = {"e4m3": (ml_dtypes.float8_e4m3fn, 7), "e5m2": (ml_dtypes.float8_e5m2, 14)}[fmt]
    v = np.moveaxis(np.asarray(x, np.float32).astype(ml_dtypes.bfloat16).astype(np.float64), axis, -1)
    blocks = v.reshape(v.shape[:-1] + (-1, 32))
    amax = np.abs(blocks).max(-1, keepdims=True)
    byte = np.maximum(np.where(amax > 0, np.frexp(amax)[1] - 1 + 127, 0) - down, 1)
    scale = np.exp2(byte - 127.0)
    codes = (blocks / scale).astype(np.float32).astype(dtype).astype(np.float64)
    return np.moveaxis((codes * scale).reshape(v.shape), -1, axis)


WIDE = False


def mx_kscale(k):
    if not WIDE:
        return np.ones(k)
    levels = np.array([10, -10, 5, -5, 0])
    a = np.random.permutation(np.resize(levels, k // 512 * 4)).reshape(k // 512, 4)
    idx = np.arange(k)
    return np.exp2(a[idx // 512, idx % 128 // 32])


BF16 = ml_dtypes.bfloat16


def bf(x):
    return np.asarray(x, np.float32).astype(BF16)


def f64(x):
    return np.asarray(x).astype(np.float64)


N, T, D, B0, C, P0, V1, P1, V2 = 2, 128, 8192, 1022, 2, 512, 2048, 512, 1024
MU = 0.25
SIG = 2.0


def softmax(v):
    e = np.exp(v - v.max(-1, keepdims=True))
    return e / e.sum(-1, keepdims=True)


def setup_inputs():
    s, t = mx_kscale(D), mx_kscale(P0)
    hw = np.random.standard_normal((D, B0 + C)) * SIG / np.sqrt(D)
    hw[:, B0:] = hw[:, B0:] / SIG + (np.log(B0) + 0.5 * SIG * SIG) / (MU * D)
    return {"x": bf((np.random.standard_normal((N, T, D)) + MU) * s),
            "head_weight": bf(hw / s[:, None]),
            "tail_proj_0": bf(np.random.standard_normal((D, P0)) / np.sqrt(D) / s[:, None] * t),
            "tail_w_0": bf(np.random.standard_normal((P0, V1)) * SIG / np.sqrt(P0) / t[:, None])}


def reference(x, head_weight, tail_proj_0, tail_w_0):
    xq = mxq(f64(x), 2, "e4m3")
    head_sm = softmax(xq @ mxq(f64(head_weight), 0, "e4m3"))
    h = xq @ mxq(f64(tail_proj_0), 0, "e4m3")
    tail_sm = softmax(mxq(h, 2, "e4m3") @ mxq(f64(tail_w_0), 0, "e4m3"))
    probs = np.concatenate([head_sm[..., :B0], tail_sm * head_sm[..., B0:B0 + 1]], axis=-1)
    return probs, head_sm[..., B0 + 1:B0 + C]

@@ -1,0 +1,380 @@
+from contextlib import ExitStack
+
+import concourse.mybir as mybir
+from concourse.masks import make_identity
+
+F32 = mybir.dt.float32
+BF16 = mybir.dt.bfloat16
+U32 = mybir.dt.uint32
+U8 = mybir.dt.uint8
+FP8X4 = mybir.dt.float8_e4m3fn_x4
+EXP = mybir.ActivationFunctionType.Exp
+COPY = mybir.ActivationFunctionType.Copy
+MULT = mybir.AluOpType.mult
+MAX = mybir.AluOpType.max
+ALONG_ROW = mybir.AxisListType.X
+
+P = 128
+PACK = 4
+K_PASS = P * PACK
+BANK = 512
+
+TOKEN_TILES = 2
+TOKENS = TOKEN_TILES * P
+D = 8192
+PASSES = D // K_PASS
+HEAD = 1024
+HEAD_TOKENS = 1022
+PROJ = 512
+TAIL = 2048
+
+BLOCKS = 2
+CHUNK = BLOCKS * BANK
+X_PASSES = 4
+STORE_COLUMNS = 1024
+RUN = 4
+
+FLOPS = 2 * TOKENS * D * (HEAD + PROJ) + 2 * TOKENS * PROJ * TAIL
+
+
+def tile_adaptiveinputsoftmax_pa_k_kernel(
+    tc, x, head_weight, tail_proj_0, tail_w_0, out_0, out_1
+):
+    nc = tc.nc
+    with ExitStack() as ctx:
+        ctx.enter_context(tc.manual_schedule())
+        keep = ctx.enter_context(tc.tile_pool(name="keep", bufs=1))
+        x_pool = ctx.enter_context(tc.tile_pool(name="x_pool", bufs=4))
+        x_grouped_pool = ctx.enter_context(tc.tile_pool(name="x_grouped_pool", bufs=2))
+        raw_pool = ctx.enter_context(tc.tile_pool(name="raw_pool", bufs=8))
+        grouped_pool = ctx.enter_context(tc.tile_pool(name="grouped_pool", bufs=3))
+        codes_pool = ctx.enter_context(tc.tile_pool(name="codes_pool", bufs=4))
+        psum = ctx.enter_context(tc.psum_pool(name="psum", bufs=1))
+
+        def bank(index, name):
+            return psum.tile([P, BANK], F32, tag="bank%d" % index, name=name)[:]
+
+        identity = keep.tile([P, P], F32, name="identity")
+        make_identity(nc, identity[:])
+        zero = keep.tile([P, 1], F32, name="zero")
+        one = keep.tile([P, 1], F32, name="one")
+        nc.vector.memset(zero[:], 0.0)
+        nc.scalar.activation(out=one[:], in_=zero[:], func=EXP)
+        cluster1 = keep.tile([P, P], F32, name="cluster1")
+        nc.vector.memset(cluster1[:], 0.0)
+
+        x_codes = keep.tile([P, PASSES * TOKENS], U32, align_bytes=64, name="x_codes")
+        x_scales = keep.tile([P, PASSES * TOKENS], U8, align_bytes=64, name="x_scales")
+
+        def transpose_x(a):
+            columns = slice(X_PASSES * K_PASS * a, X_PASSES * K_PASS * (a + 1))
+            words = []
+            for m in range(TOKEN_TILES):
+                x_raw = x_pool.tile([P, X_PASSES * K_PASS], BF16, name="x_raw")
+                nc.sync.dma_start(out=x_raw[:], in_=x[m, :, columns])
+                words.append(
+                    x_raw[:].bitcast(F32).rearrange("r (g p u) -> r g u p", g=X_PASSES, u=2)
+                )
+            x_grouped = x_grouped_pool.tile(
+                [P, X_PASSES * TOKENS * PACK], BF16, align_bytes=64, name="x_grouped"
+            )
+            grouped_words = x_grouped[:].bitcast(F32).rearrange(
+                "p (g r u) -> p g r u", g=X_PASSES, u=2
+            )
+            for g in range(X_PASSES):
+                xt = bank(g, "xt").rearrange("p (u r) -> p u r", u=2)
+                for u in range(2):
+                    for m in range(TOKEN_TILES):
+                        nc.tensor.transpose(
+                            xt[:, u, P * m : P * (m + 1)], words[m][:, g, u, :], identity[:]
+                        )
+                nc.scalar.copy(out=grouped_words[:, g], in_=xt.rearrange("p u r -> p r u"))
+            return x_grouped
+
+        def quantise_x(a, x_grouped):
+            columns = slice(X_PASSES * TOKENS * a, X_PASSES * TOKENS * (a + 1))
+            nc.vector.quantize_mx(
+                out=x_codes[:, columns].bitcast(FP8X4),
+                scales=x_scales[:, columns],
+                in_=x_grouped[:],
+            )
+
+        previous = {}
+
+        def finish_previous():
+            job = previous.get("job")
+            if job is not None:
+                grouped, codes, scales, multiply, index = job
+                nc.vector.quantize_mx(out=codes.bitcast(FP8X4), scales=scales, in_=grouped[:])
+                if multiply is not None:
+                    multiply(index, codes, scales)
+            previous["job"] = None
+
+        def step(raw_blocks, codes, scales, multiply, index):
+            grouped = grouped_pool.tile([P, CHUNK * PACK], BF16, align_bytes=64, name="grouped")
+            blocks = grouped[:].rearrange("p (b w t) -> p b w t", b=BLOCKS, t=PACK)
+            for b, copy in enumerate((nc.vector.tensor_copy, nc.scalar.copy)):
+                copy(
+                    out=blocks[:, b].rearrange("p (c i) t -> p c t i", i=RUN),
+                    in_=raw_blocks[b].rearrange("p t (c i) -> p c t i", i=RUN),
+                )
+            finish_previous()
+            previous["job"] = (grouped, codes, scales, multiply, index)
+
+        def new_codes():
+            codes = codes_pool.tile([P, CHUNK], U32, align_bytes=64, name="codes")
+            scales = codes_pool.tile([P, CHUNK], U8, align_bytes=64, name="scales")
+            return codes[:], scales[:]
+
+        QUARTERS = PROJ // P
+        h_acc = [bank(4 + q, "h_acc%d" % q) for q in range(QUARTERS)]
+
+        def project(j, codes, scales):
+            for b in range(BLOCKS):
+                c = BLOCKS * j + b
+                tokens = slice(TOKENS * c, TOKENS * (c + 1))
+                for q in range(QUARTERS):
+                    columns = slice(BANK * b + P * q, BANK * b + P * (q + 1))
+                    nc.tensor.matmul_mx(
+                        out=h_acc[q][:, 0:TOKENS],
+                        lhsT=codes[:, columns].bitcast(FP8X4),
+                        lhsT_scale=scales[:, columns],
+                        rhs=x_codes[:, tokens].bitcast(FP8X4),
+                        rhs_scale=x_scales[:, tokens],
+                        start=(c == 0),
+                        stop=(c == PASSES - 1),
+                    )
+
+        for j in range(PASSES // BLOCKS):
+            new_x = (BLOCKS * j) % X_PASSES == 0
+            if new_x:
+                a = BLOCKS * j // X_PASSES
+                x_grouped = transpose_x(a)
+            raw = raw_pool.tile([P, CHUNK * PACK], BF16, name="raw")
+            passes = raw[:].rearrange("p (c t w) -> p c t w", c=BLOCKS, t=PACK)
+            rows = tail_proj_0[BLOCKS * K_PASS * j : BLOCKS * K_PASS * (j + 1), :]
+            nc.sync.dma_start(
+                out=passes, in_=rows.rearrange("(c p t) w -> p c t w", c=BLOCKS, t=PACK)
+            )
+            codes, scales = new_codes()
+            step([passes[:, b] for b in range(BLOCKS)], codes, scales, project, j)
+            if new_x:
+                quantise_x(a, x_grouped)
+
+        tail_codes = keep.tile([P, TAIL], U32, align_bytes=64, name="tail_codes")
+        tail_scales = keep.tile([P, TAIL], U8, align_bytes=64, name="tail_scales")
+        tail_rows = tail_w_0.rearrange("(t p) n -> p t n", p=P)
+        for i in range(TAIL // CHUNK):
+            columns = slice(CHUNK * i, CHUNK * (i + 1))
+            raw = raw_pool.tile([P, CHUNK * PACK], BF16, name="raw")
+            rows = raw[:].rearrange("p (t w) -> p t w", t=PACK)
+            nc.sync.dma_start(out=rows, in_=tail_rows[:, :, columns])
+            step(
+                [rows[:, :, BANK * b : BANK * (b + 1)] for b in range(BLOCKS)],
+                tail_codes[:, columns],
+                tail_scales[:, columns],
+                None,
+                i,
+            )
+
+        h_rounded = keep.tile([P, QUARTERS, TOKENS], BF16, name="h_rounded")
+        h_grouped = keep.tile([P, TOKENS, PACK], BF16, align_bytes=64, name="h_grouped")
+        h_codes = keep.tile([P, TOKENS], U32, align_bytes=64, name="h_codes")
+        h_scales = keep.tile([P, TOKENS], U8, align_bytes=64, name="h_scales")
+        TAIL_BANKS = TAIL // BANK
+        tail_logits = {}
+        tail_exp = [keep.tile([P, TAIL], F32, name="tail_exp%d" % m) for m in range(TOKEN_TILES)]
+        tail_bank_max = [
+            keep.tile([P, TAIL_BANKS], F32, name="tail_bank_max%d" % m) for m in range(TOKEN_TILES)
+        ]
+        tail_neg_max = [keep.tile([P, 1], F32, name="tail_neg_max%d" % m) for m in range(TOKEN_TILES)]
+        tail_bank_sum = [
+            keep.tile([P, TAIL_BANKS], F32, name="tail_bank_sum%d" % m) for m in range(TOKEN_TILES)
+        ]
+        tail_sum = [keep.tile([P, 1], F32, name="tail_sum%d" % m) for m in range(TOKEN_TILES)]
+        tail_inverse = [keep.tile([P, 1], F32, name="tail_inverse%d" % m) for m in range(TOKEN_TILES)]
+
+        def round_h():
+            for q in range(QUARTERS):
+                copy = nc.vector.tensor_copy if q % 2 == 0 else nc.scalar.copy
+                copy(out=h_rounded[:, q, :], in_=h_acc[q][:, 0:TOKENS])
+
+        def regroup_h():
+            nc.vector.tensor_copy(
+                out=h_grouped[:].rearrange("p (c i) t -> p c t i", i=RUN),
+                in_=h_rounded[:].rearrange("p t (c i) -> p c t i", i=RUN),
+            )
+
+        def quantise_h():
+            nc.vector.quantize_mx(
+                out=h_codes[:].bitcast(FP8X4),
+                scales=h_scales[:],
+                in_=h_grouped[:].rearrange("p r t -> p (r t)"),
+            )
+
+        def multiply_tail(m):
+            tokens = slice(P * m, P * (m + 1))
+            for n in range(TAIL_BANKS):
+                columns = slice(BANK * n, BANK * (n + 1))
+                tail_logits[(m, n)] = bank(4 + n, "tail_logits")
+                nc.tensor.matmul_mx(
+                    out=tail_logits[(m, n)],
+                    lhsT=h_codes[:, tokens].bitcast(FP8X4),
+                    lhsT_scale=h_scales[:, tokens],
+                    rhs=tail_codes[:, columns].bitcast(FP8X4),
+                    rhs_scale=tail_scales[:, columns],
+                    start=True,
+                    stop=True,
+                )
+
+        def max_tail(m):
+            for n in range(TAIL_BANKS):
+                nc.vector.reduce_max(
+                    out=tail_bank_max[m][:, n : n + 1], in_=tail_logits[(m, n)], axis=ALONG_ROW
+                )
+            nc.vector.tensor_reduce(
+                out=tail_neg_max[m][:], in_=tail_bank_max[m][:], axis=ALONG_ROW, op=MAX, negate=True
+            )
+
+        def exp_tail(m):
+            for n in range(TAIL_BANKS):
+                nc.scalar.activation(
+                    out=tail_exp[m][:, BANK * n : BANK * (n + 1)],
+                    in_=tail_logits[(m, n)],
+                    func=EXP,
+                    bias=tail_neg_max[m][:],
+                    accum_out=tail_bank_sum[m][:, n : n + 1],
+                )
+
+        def invert_tail_sum(m):
+            nc.vector.reduce_sum(out=tail_sum[m][:], in_=tail_bank_sum[m][:], axis=ALONG_ROW)
+            nc.vector.reciprocal(out=tail_inverse[m][:], in_=tail_sum[m][:])
+
+        tail_stages = [round_h, regroup_h, quantise_h]
+        for m in range(TOKEN_TILES):
+            tail_stages.extend(
+                [
+                    lambda m=m: multiply_tail(m),
+                    lambda m=m: max_tail(m),
+                    lambda m=m: exp_tail(m),
+                    lambda m=m: invert_tail_sum(m),
+                ]
+            )
+
+        HEAD_BANKS = HEAD // BANK
+        head_acc = [
+            [bank(HEAD_BANKS * m + n, "head_acc%d%d" % (m, n)) for n in range(HEAD_BANKS)]
+            for m in range(TOKEN_TILES)
+        ]
+
+        def multiply_head(c, codes, scales):
+            for m in range(TOKEN_TILES):
+                tokens = slice(TOKENS * c + P * m, TOKENS * c + P * (m + 1))
+                for n in range(HEAD_BANKS):
+                    columns = slice(BANK * n, BANK * (n + 1))
+                    nc.tensor.matmul_mx(
+                        out=head_acc[m][n],
+                        lhsT=x_codes[:, tokens].bitcast(FP8X4),
+                        lhsT_scale=x_scales[:, tokens],
+                        rhs=codes[:, columns].bitcast(FP8X4),
+                        rhs_scale=scales[:, columns],
+                        start=(c == 0),
+                        stop=(c == PASSES - 1),
+                    )
+
+        for c in range(PASSES):
+            raw = raw_pool.tile([P, CHUNK * PACK], BF16, name="raw")
+            rows = raw[:].rearrange("p (t w) -> p t w", t=PACK)
+            nc.sync.dma_start(
+                out=rows,
+                in_=head_weight[K_PASS * c : K_PASS * (c + 1), :].rearrange(
+                    "(p t) w -> p t w", t=PACK
+                ),
+            )
+            codes, scales = new_codes()
+            step(
+                [rows[:, :, BANK * b : BANK * (b + 1)] for b in range(BLOCKS)],
+                codes,
+                scales,
+                multiply_head,
+                c,
+            )
+            if c < len(tail_stages):
+                tail_stages[c]()
+        finish_previous()
+
+        head_exp = [keep.tile([P, HEAD], F32, name="head_exp%d" % m) for m in range(TOKEN_TILES)]
+        head_bank_max = [
+            keep.tile([P, HEAD_BANKS], F32, name="head_bank_max%d" % m) for m in range(TOKEN_TILES)
+        ]
+        head_neg_max = [keep.tile([P, 1], F32, name="head_neg_max%d" % m) for m in range(TOKEN_TILES)]
+        head_bank_sum = [
+            keep.tile([P, HEAD_BANKS], F32, name="head_bank_sum%d" % m) for m in range(TOKEN_TILES)
+        ]
+        head_sum = [keep.tile([P, 1], F32, name="head_sum%d" % m) for m in range(TOKEN_TILES)]
+        head_inverse = [keep.tile([P, 1], F32, name="head_inverse%d" % m) for m in range(TOKEN_TILES)]
+        tail_factor = [keep.tile([P, 1], F32, name="tail_factor%d" % m) for m in range(TOKEN_TILES)]
+
+        for m in range(TOKEN_TILES):
+            for n in range(HEAD_BANKS):
+                nc.vector.reduce_max(
+                    out=head_bank_max[m][:, n : n + 1], in_=head_acc[m][n], axis=ALONG_ROW
+                )
+            nc.vector.tensor_reduce(
+                out=head_neg_max[m][:], in_=head_bank_max[m][:], axis=ALONG_ROW, op=MAX, negate=True
+            )
+        for m in range(TOKEN_TILES):
+            for n in range(HEAD_BANKS):
+                nc.scalar.activation(
+                    out=head_exp[m][:, BANK * n : BANK * (n + 1)],
+                    in_=head_acc[m][n],
+                    func=EXP,
+                    bias=head_neg_max[m][:],
+                    accum_out=head_bank_sum[m][:, n : n + 1],
+                )
+        for m in range(TOKEN_TILES):
+            nc.vector.reduce_sum(out=head_sum[m][:], in_=head_bank_sum[m][:], axis=ALONG_ROW)
+            nc.vector.reciprocal(out=head_inverse[m][:], in_=head_sum[m][:])
+            nc.vector.tensor_scalar(
+                out=tail_factor[m][:],
+                in0=head_exp[m][:, HEAD_TOKENS : HEAD_TOKENS + 1],
+                scalar1=head_inverse[m][:],
+                scalar2=tail_inverse[m][:],
+                op0=MULT,
+                op1=MULT,
+            )
+            nc.vector.tensor_scalar(
+                out=cluster1[:, m : m + 1],
+                in0=head_exp[m][:, HEAD_TOKENS + 1 : HEAD_TOKENS + 2],
+                scalar1=head_inverse[m][:],
+                scalar2=None,
+                op0=MULT,
+            )
+            for first in range(0, TAIL, STORE_COLUMNS):
+                columns = slice(first, first + STORE_COLUMNS)
+                nc.vector.tensor_scalar(
+                    out=tail_exp[m][:, columns],
+                    in0=tail_exp[m][:, columns],
+                    scalar1=tail_factor[m][:],
+                    scalar2=None,
+                    op0=MULT,
+                )
+                nc.sync.dma_start(
+                    out=out_0[m, :, HEAD_TOKENS + first : HEAD_TOKENS + first + STORE_COLUMNS],
+                    in_=tail_exp[m][:, columns],
+                )
+            nc.scalar.activation(
+                out=head_exp[m][:, 0:HEAD_TOKENS],
+                in_=head_exp[m][:, 0:HEAD_TOKENS],
+                func=COPY,
+                scale=head_inverse[m][:],
+            )
+            nc.sync.dma_start(out=out_0[m, :, 0:HEAD_TOKENS], in_=head_exp[m][:, 0:HEAD_TOKENS])
+
+        cluster1_rows = bank(4, "cluster1_rows")
+        nc.tensor.transpose(cluster1_rows[:, 0:P], cluster1[:], identity[:])
+        cluster1_out = keep.tile([P, P], F32, name="cluster1_out")
+        nc.scalar.copy(out=cluster1_out[:], in_=cluster1_rows[:, 0:P])
+        nc.sync.dma_start(
+            out=out_1.rearrange("n t o -> n (t o)"), in_=cluster1_out[0:TOKEN_TILES, :]
+        )

@@ -32,6 +32,8 @@ BLOCKS = 2
 CHUNK = BLOCKS * BANK
 X_PASSES = 4
 STORE_COLUMNS = 1024
+LAG = 2
+VECTOR_COLUMNS = 448
 RUN = 4
 
 FLOPS = 2 * TOKENS * D * (HEAD + PROJ) + 2 * TOKENS * PROJ * TAIL
@@ -42,13 +44,12 @@ def tile_adaptiveinputsoftmax_pa_k_kernel(
 ):
     nc = tc.nc
     with ExitStack() as ctx:
-        ctx.enter_context(tc.manual_schedule())
         keep = ctx.enter_context(tc.tile_pool(name="keep", bufs=1))
         x_pool = ctx.enter_context(tc.tile_pool(name="x_pool", bufs=4))
         x_grouped_pool = ctx.enter_context(tc.tile_pool(name="x_grouped_pool", bufs=2))
         raw_pool = ctx.enter_context(tc.tile_pool(name="raw_pool", bufs=8))
-        grouped_pool = ctx.enter_context(tc.tile_pool(name="grouped_pool", bufs=3))
-        codes_pool = ctx.enter_context(tc.tile_pool(name="codes_pool", bufs=4))
+        grouped_pool = ctx.enter_context(tc.tile_pool(name="grouped_pool", bufs=LAG + 2))
+        codes_pool = ctx.enter_context(tc.tile_pool(name="codes_pool", bufs=3))
         psum = ctx.enter_context(tc.psum_pool(name="psum", bufs=1))
 
         def bank(index, name):
@@ -99,32 +100,38 @@ def tile_adaptiveinputsoftmax_pa_k_kernel(
                 in_=x_grouped[:],
             )
 
-        previous = {}
+        regrouped = []
 
-        def finish_previous():
-            job = previous.get("job")
-            if job is not None:
-                grouped, codes, scales, multiply, index = job
-                nc.vector.quantize_mx(out=codes.bitcast(FP8X4), scales=scales, in_=grouped[:])
-                if multiply is not None:
-                    multiply(index, codes, scales)
-            previous["job"] = None
+        def quantise_and_multiply(job):
+            grouped, codes, scales, multiply, index = job
+            if codes is None:
+                codes = codes_pool.tile([P, CHUNK], U32, align_bytes=64, name="codes")[:]
+                scales = codes_pool.tile([P, CHUNK], U8, align_bytes=64, name="scales")[:]
+            nc.vector.quantize_mx(
+                out=codes.bitcast(FP8X4),
+                scales=scales,
+                in_=grouped[:].rearrange("p w t -> p (w t)"),
+            )
+            if multiply is not None:
+                multiply(index, codes, scales)
 
-        def step(raw_blocks, codes, scales, multiply, index):
-            grouped = grouped_pool.tile([P, CHUNK * PACK], BF16, align_bytes=64, name="grouped")
-            blocks = grouped[:].rearrange("p (b w t) -> p b w t", b=BLOCKS, t=PACK)
-            for b, copy in enumerate((nc.vector.tensor_copy, nc.scalar.copy)):
+        def step(vector_part, scalar_part, codes, scales, multiply, index):
+            grouped = grouped_pool.tile([P, CHUNK, PACK], BF16, align_bytes=64, name="grouped")
+            for copy, (raw_part, first) in (
+                (nc.vector.tensor_copy, vector_part),
+                (nc.scalar.copy, scalar_part),
+            ):
+                columns = grouped[:, first : first + raw_part.shape[2], :]
                 copy(
-                    out=blocks[:, b].rearrange("p (c i) t -> p c t i", i=RUN),
-                    in_=raw_blocks[b].rearrange("p t (c i) -> p c t i", i=RUN),
+                    out=columns.rearrange("p (c i) t -> p c t i", i=RUN),
+                    in_=raw_part.rearrange("p t (c i) -> p c t i", i=RUN),
                 )
-            finish_previous()
-            previous["job"] = (grouped, codes, scales, multiply, index)
+            regrouped.append((grouped, codes, scales, multiply, index))
+            if len(regrouped) > LAG:
+                quantise_and_multiply(regrouped[-1 - LAG])
 
-        def new_codes():
-            codes = codes_pool.tile([P, CHUNK], U32, align_bytes=64, name="codes")
-            scales = codes_pool.tile([P, CHUNK], U8, align_bytes=64, name="scales")
-            return codes[:], scales[:]
+        def split_columns(rows):
+            return (rows[:, :, 0:VECTOR_COLUMNS], 0), (rows[:, :, VECTOR_COLUMNS:CHUNK], VECTOR_COLUMNS)
 
         QUARTERS = PROJ // P
         h_acc = [bank(4 + q, "h_acc%d" % q) for q in range(QUARTERS)]
@@ -145,21 +152,23 @@ def tile_adaptiveinputsoftmax_pa_k_kernel(
                         stop=(c == PASSES - 1),
                     )
 
+        X_PERIOD = X_PASSES // BLOCKS
         for j in range(PASSES // BLOCKS):
-            new_x = (BLOCKS * j) % X_PASSES == 0
-            if new_x:
-                a = BLOCKS * j // X_PASSES
-                x_grouped = transpose_x(a)
             raw = raw_pool.tile([P, CHUNK * PACK], BF16, name="raw")
             passes = raw[:].rearrange("p (c t w) -> p c t w", c=BLOCKS, t=PACK)
-            rows = tail_proj_0[BLOCKS * K_PASS * j : BLOCKS * K_PASS * (j + 1), :]
-            nc.sync.dma_start(
-                out=passes, in_=rows.rearrange("(c p t) w -> p c t w", c=BLOCKS, t=PACK)
-            )
-            codes, scales = new_codes()
-            step([passes[:, b] for b in range(BLOCKS)], codes, scales, project, j)
-            if new_x:
-                quantise_x(a, x_grouped)
+            for b in range(BLOCKS):
+                c = BLOCKS * j + b
+                nc.sync.dma_start(
+                    out=passes[:, b],
+                    in_=tail_proj_0[K_PASS * c : K_PASS * (c + 1), :].rearrange(
+                        "(p t) w -> p t w", t=PACK
+                    ),
+                )
+            step((passes[:, 0], 0), (passes[:, 1], BANK), None, None, project, j)
+            if j % X_PERIOD == 0:
+                x_grouped = transpose_x(j // X_PERIOD)
+            if j % X_PERIOD == 1:
+                quantise_x(j // X_PERIOD, x_grouped)
 
         tail_codes = keep.tile([P, TAIL], U32, align_bytes=64, name="tail_codes")
         tail_scales = keep.tile([P, TAIL], U8, align_bytes=64, name="tail_scales")
@@ -169,13 +178,8 @@ def tile_adaptiveinputsoftmax_pa_k_kernel(
             raw = raw_pool.tile([P, CHUNK * PACK], BF16, name="raw")
             rows = raw[:].rearrange("p (t w) -> p t w", t=PACK)
             nc.sync.dma_start(out=rows, in_=tail_rows[:, :, columns])
-            step(
-                [rows[:, :, BANK * b : BANK * (b + 1)] for b in range(BLOCKS)],
-                tail_codes[:, columns],
-                tail_scales[:, columns],
-                None,
-                i,
-            )
+            vector_part, scalar_part = split_columns(rows)
+            step(vector_part, scalar_part, tail_codes[:, columns], tail_scales[:, columns], None, i)
 
         h_rounded = keep.tile([P, QUARTERS, TOKENS], BF16, name="h_rounded")
         h_grouped = keep.tile([P, TOKENS, PACK], BF16, align_bytes=64, name="h_grouped")
@@ -291,17 +295,12 @@ def tile_adaptiveinputsoftmax_pa_k_kernel(
                     "(p t) w -> p t w", t=PACK
                 ),
             )
-            codes, scales = new_codes()
-            step(
-                [rows[:, :, BANK * b : BANK * (b + 1)] for b in range(BLOCKS)],
-                codes,
-                scales,
-                multiply_head,
-                c,
-            )
+            vector_part, scalar_part = split_columns(rows)
+            step(vector_part, scalar_part, None, None, multiply_head, c)
             if c < len(tail_stages):
                 tail_stages[c]()
-        finish_previous()
+        for job in regrouped[-LAG:]:
+            quantise_and_multiply(job)
 
         head_exp = [keep.tile([P, HEAD], F32, name="head_exp%d" % m) for m in range(TOKEN_TILES)]
         head_bank_max = [

@@ -33,7 +33,7 @@ CHUNK = BLOCKS * BANK
 X_PASSES = 4
 STORE_COLUMNS = 1024
 LAG = 2
-VECTOR_COLUMNS = 448
+PIECE = 256
 RUN = 4
 
 FLOPS = 2 * TOKENS * D * (HEAD + PROJ) + 2 * TOKENS * PROJ * TAIL
@@ -115,23 +115,19 @@ def tile_adaptiveinputsoftmax_pa_k_kernel(
             if multiply is not None:
                 multiply(index, codes, scales)
 
-        def step(vector_part, scalar_part, codes, scales, multiply, index):
+        def step(pieces, codes, scales, multiply, index):
             grouped = grouped_pool.tile([P, CHUNK, PACK], BF16, align_bytes=64, name="grouped")
-            for copy, (raw_part, first) in (
-                (nc.vector.tensor_copy, vector_part),
-                (nc.scalar.copy, scalar_part),
-            ):
-                columns = grouped[:, first : first + raw_part.shape[2], :]
-                copy(
-                    out=columns.rearrange("p (c i) t -> p c t i", i=RUN),
-                    in_=raw_part.rearrange("p t (c i) -> p c t i", i=RUN),
+            for raw_piece, first in pieces:
+                nc.any.tensor_copy(
+                    out=grouped[:, first : first + PIECE, :].rearrange("p (c i) t -> p c t i", i=RUN),
+                    in_=raw_piece.rearrange("p t (c i) -> p c t i", i=RUN),
                 )
             regrouped.append((grouped, codes, scales, multiply, index))
             if len(regrouped) > LAG:
                 quantise_and_multiply(regrouped[-1 - LAG])
 
-        def split_columns(rows):
-            return (rows[:, :, 0:VECTOR_COLUMNS], 0), (rows[:, :, VECTOR_COLUMNS:CHUNK], VECTOR_COLUMNS)
+        def column_pieces(rows):
+            return [(rows[:, :, first : first + PIECE], first) for first in range(0, CHUNK, PIECE)]
 
         QUARTERS = PROJ // P
         h_acc = [bank(4 + q, "h_acc%d" % q) for q in range(QUARTERS)]
@@ -164,7 +160,12 @@ def tile_adaptiveinputsoftmax_pa_k_kernel(
                         "(p t) w -> p t w", t=PACK
                     ),
                 )
-            step((passes[:, 0], 0), (passes[:, 1], BANK), None, None, project, j)
+            pieces = [
+                (passes[:, b, :, first : first + PIECE], BANK * b + first)
+                for b in range(BLOCKS)
+                for first in range(0, BANK, PIECE)
+            ]
+            step(pieces, None, None, project, j)
             if j % X_PERIOD == 0:
                 x_grouped = transpose_x(j // X_PERIOD)
             if j % X_PERIOD == 1:
@@ -178,8 +179,7 @@ def tile_adaptiveinputsoftmax_pa_k_kernel(
             raw = raw_pool.tile([P, CHUNK * PACK], BF16, name="raw")
             rows = raw[:].rearrange("p (t w) -> p t w", t=PACK)
             nc.sync.dma_start(out=rows, in_=tail_rows[:, :, columns])
-            vector_part, scalar_part = split_columns(rows)
-            step(vector_part, scalar_part, tail_codes[:, columns], tail_scales[:, columns], None, i)
+            step(column_pieces(rows), tail_codes[:, columns], tail_scales[:, columns], None, i)
 
         h_rounded = keep.tile([P, QUARTERS, TOKENS], BF16, name="h_rounded")
         h_grouped = keep.tile([P, TOKENS, PACK], BF16, align_bytes=64, name="h_grouped")
@@ -256,14 +256,9 @@ def tile_adaptiveinputsoftmax_pa_k_kernel(
 
         tail_stages = [round_h, regroup_h, quantise_h]
         for m in range(TOKEN_TILES):
-            tail_stages.extend(
-                [
-                    lambda m=m: multiply_tail(m),
-                    lambda m=m: max_tail(m),
-                    lambda m=m: exp_tail(m),
-                    lambda m=m: invert_tail_sum(m),
-                ]
-            )
+            tail_stages.extend([lambda m=m: multiply_tail(m), lambda m=m: max_tail(m)])
+            if m < TOKEN_TILES - 1:
+                tail_stages.extend([lambda m=m: exp_tail(m), lambda m=m: invert_tail_sum(m)])
 
         HEAD_BANKS = HEAD // BANK
         head_acc = [
@@ -295,12 +290,13 @@ def tile_adaptiveinputsoftmax_pa_k_kernel(
                     "(p t) w -> p t w", t=PACK
                 ),
             )
-            vector_part, scalar_part = split_columns(rows)
-            step(vector_part, scalar_part, None, None, multiply_head, c)
+            step(column_pieces(rows), None, None, multiply_head, c)
             if c < len(tail_stages):
                 tail_stages[c]()
         for job in regrouped[-LAG:]:
             quantise_and_multiply(job)
+        exp_tail(TOKEN_TILES - 1)
+        invert_tail_sum(TOKEN_TILES - 1)
 
         head_exp = [keep.tile([P, HEAD], F32, name="head_exp%d" % m) for m in range(TOKEN_TILES)]
         head_bank_max = [

from contextlib import ExitStack

import concourse.mybir as mybir
from concourse.masks import make_identity

F32 = mybir.dt.float32
BF16 = mybir.dt.bfloat16
U32 = mybir.dt.uint32
U8 = mybir.dt.uint8
FP8X4 = mybir.dt.float8_e4m3fn_x4
EXP = mybir.ActivationFunctionType.Exp
COPY = mybir.ActivationFunctionType.Copy
MULT = mybir.AluOpType.mult
MAX = mybir.AluOpType.max
ALONG_ROW = mybir.AxisListType.X

P = 128
PACK = 4
K_PASS = P * PACK
BANK = 512

TOKEN_TILES = 2
TOKENS = TOKEN_TILES * P
D = 8192
PASSES = D // K_PASS
HEAD = 1024
HEAD_TOKENS = 1022
PROJ = 512
TAIL = 2048

BLOCKS = 2
CHUNK = BLOCKS * BANK
X_PASSES = 4
STORE_COLUMNS = 1024
LAG = 2
PIECE = 256
RUN = 4

FLOPS = 2 * TOKENS * D * (HEAD + PROJ) + 2 * TOKENS * PROJ * TAIL


def tile_adaptiveinputsoftmax_pa_k_kernel(
    tc, x, head_weight, tail_proj_0, tail_w_0, out_0, out_1
):
    nc = tc.nc
    with ExitStack() as ctx:
        keep = ctx.enter_context(tc.tile_pool(name="keep", bufs=1))
        x_pool = ctx.enter_context(tc.tile_pool(name="x_pool", bufs=4))
        x_grouped_pool = ctx.enter_context(tc.tile_pool(name="x_grouped_pool", bufs=2))
        raw_pool = ctx.enter_context(tc.tile_pool(name="raw_pool", bufs=8))
        grouped_pool = ctx.enter_context(tc.tile_pool(name="grouped_pool", bufs=LAG + 2))
        codes_pool = ctx.enter_context(tc.tile_pool(name="codes_pool", bufs=3))
        psum = ctx.enter_context(tc.psum_pool(name="psum", bufs=1))

        def bank(index, name):
            return psum.tile([P, BANK], F32, tag="bank%d" % index, name=name)[:]

        identity = keep.tile([P, P], F32, name="identity")
        make_identity(nc, identity[:])
        zero = keep.tile([P, 1], F32, name="zero")
        one = keep.tile([P, 1], F32, name="one")
        nc.vector.memset(zero[:], 0.0)
        nc.scalar.activation(out=one[:], in_=zero[:], func=EXP)
        cluster1 = keep.tile([P, P], F32, name="cluster1")
        nc.vector.memset(cluster1[:], 0.0)

        x_codes = keep.tile([P, PASSES * TOKENS], U32, align_bytes=64, name="x_codes")
        x_scales = keep.tile([P, PASSES * TOKENS], U8, align_bytes=64, name="x_scales")

        def transpose_x(a):
            columns = slice(X_PASSES * K_PASS * a, X_PASSES * K_PASS * (a + 1))
            words = []
            for m in range(TOKEN_TILES):
                x_raw = x_pool.tile([P, X_PASSES * K_PASS], BF16, name="x_raw")
                nc.sync.dma_start(out=x_raw[:], in_=x[m, :, columns])
                words.append(
                    x_raw[:].bitcast(F32).rearrange("r (g p u) -> r g u p", g=X_PASSES, u=2)
                )
            x_grouped = x_grouped_pool.tile(
                [P, X_PASSES * TOKENS * PACK], BF16, align_bytes=64, name="x_grouped"
            )
            grouped_words = x_grouped[:].bitcast(F32).rearrange(
                "p (g r u) -> p g r u", g=X_PASSES, u=2
            )
            for g in range(X_PASSES):
                xt = bank(g, "xt").rearrange("p (u r) -> p u r", u=2)
                for u in range(2):
                    for m in range(TOKEN_TILES):
                        nc.tensor.transpose(
                            xt[:, u, P * m : P * (m + 1)], words[m][:, g, u, :], identity[:]
                        )
                nc.scalar.copy(out=grouped_words[:, g], in_=xt.rearrange("p u r -> p r u"))
            return x_grouped

        def quantise_x(a, x_grouped):
            columns = slice(X_PASSES * TOKENS * a, X_PASSES * TOKENS * (a + 1))
            nc.vector.quantize_mx(
                out=x_codes[:, columns].bitcast(FP8X4),
                scales=x_scales[:, columns],
                in_=x_grouped[:],
            )

        regrouped = []

        def quantise_and_multiply(job):
            grouped, codes, scales, multiply, index = job
            if codes is None:
                codes = codes_pool.tile([P, CHUNK], U32, align_bytes=64, name="codes")[:]
                scales = codes_pool.tile([P, CHUNK], U8, align_bytes=64, name="scales")[:]
            nc.vector.quantize_mx(
                out=codes.bitcast(FP8X4),
                scales=scales,
                in_=grouped[:].rearrange("p w t -> p (w t)"),
            )
            if multiply is not None:
                multiply(index, codes, scales)

        def step(pieces, codes, scales, multiply, index):
            grouped = grouped_pool.tile([P, CHUNK, PACK], BF16, align_bytes=64, name="grouped")
            for raw_piece, first in pieces:
                nc.any.tensor_copy(
                    out=grouped[:, first : first + PIECE, :].rearrange("p (c i) t -> p c t i", i=RUN),
                    in_=raw_piece.rearrange("p t (c i) -> p c t i", i=RUN),
                )
            regrouped.append((grouped, codes, scales, multiply, index))
            if len(regrouped) > LAG:
                quantise_and_multiply(regrouped[-1 - LAG])

        def column_pieces(rows):
            return [(rows[:, :, first : first + PIECE], first) for first in range(0, CHUNK, PIECE)]

        QUARTERS = PROJ // P
        h_acc = [bank(4 + q, "h_acc%d" % q) for q in range(QUARTERS)]

        def project(j, codes, scales):
            for b in range(BLOCKS):
                c = BLOCKS * j + b
                tokens = slice(TOKENS * c, TOKENS * (c + 1))
                for q in range(QUARTERS):
                    columns = slice(BANK * b + P * q, BANK * b + P * (q + 1))
                    nc.tensor.matmul_mx(
                        out=h_acc[q][:, 0:TOKENS],
                        lhsT=codes[:, columns].bitcast(FP8X4),
                        lhsT_scale=scales[:, columns],
                        rhs=x_codes[:, tokens].bitcast(FP8X4),
                        rhs_scale=x_scales[:, tokens],
                        start=(c == 0),
                        stop=(c == PASSES - 1),
                    )

        X_PERIOD = X_PASSES // BLOCKS
        for j in range(PASSES // BLOCKS):
            raw = raw_pool.tile([P, CHUNK * PACK], BF16, name="raw")
            passes = raw[:].rearrange("p (c t w) -> p c t w", c=BLOCKS, t=PACK)
            for b in range(BLOCKS):
                c = BLOCKS * j + b
                nc.sync.dma_start(
                    out=passes[:, b],
                    in_=tail_proj_0[K_PASS * c : K_PASS * (c + 1), :].rearrange(
                        "(p t) w -> p t w", t=PACK
                    ),
                )
            pieces = [
                (passes[:, b, :, first : first + PIECE], BANK * b + first)
                for b in range(BLOCKS)
                for first in range(0, BANK, PIECE)
            ]
            step(pieces, None, None, project, j)
            if j % X_PERIOD == 0:
                x_grouped = transpose_x(j // X_PERIOD)
            if j % X_PERIOD == 1:
                quantise_x(j // X_PERIOD, x_grouped)

        tail_codes = keep.tile([P, TAIL], U32, align_bytes=64, name="tail_codes")
        tail_scales = keep.tile([P, TAIL], U8, align_bytes=64, name="tail_scales")
        tail_rows = tail_w_0.rearrange("(t p) n -> p t n", p=P)
        for i in range(TAIL // CHUNK):
            columns = slice(CHUNK * i, CHUNK * (i + 1))
            raw = raw_pool.tile([P, CHUNK * PACK], BF16, name="raw")
            rows = raw[:].rearrange("p (t w) -> p t w", t=PACK)
            nc.sync.dma_start(out=rows, in_=tail_rows[:, :, columns])
            step(column_pieces(rows), tail_codes[:, columns], tail_scales[:, columns], None, i)

        h_rounded = keep.tile([P, QUARTERS, TOKENS], BF16, name="h_rounded")
        h_grouped = keep.tile([P, TOKENS, PACK], BF16, align_bytes=64, name="h_grouped")
        h_codes = keep.tile([P, TOKENS], U32, align_bytes=64, name="h_codes")
        h_scales = keep.tile([P, TOKENS], U8, align_bytes=64, name="h_scales")
        TAIL_BANKS = TAIL // BANK
        tail_logits = {}
        tail_exp = [keep.tile([P, TAIL], F32, name="tail_exp%d" % m) for m in range(TOKEN_TILES)]
        tail_bank_max = [
            keep.tile([P, TAIL_BANKS], F32, name="tail_bank_max%d" % m) for m in range(TOKEN_TILES)
        ]
        tail_neg_max = [keep.tile([P, 1], F32, name="tail_neg_max%d" % m) for m in range(TOKEN_TILES)]
        tail_bank_sum = [
            keep.tile([P, TAIL_BANKS], F32, name="tail_bank_sum%d" % m) for m in range(TOKEN_TILES)
        ]
        tail_sum = [keep.tile([P, 1], F32, name="tail_sum%d" % m) for m in range(TOKEN_TILES)]
        tail_inverse = [keep.tile([P, 1], F32, name="tail_inverse%d" % m) for m in range(TOKEN_TILES)]

        def round_h():
            for q in range(QUARTERS):
                copy = nc.vector.tensor_copy if q % 2 == 0 else nc.scalar.copy
                copy(out=h_rounded[:, q, :], in_=h_acc[q][:, 0:TOKENS])

        def regroup_h():
            nc.vector.tensor_copy(
                out=h_grouped[:].rearrange("p (c i) t -> p c t i", i=RUN),
                in_=h_rounded[:].rearrange("p t (c i) -> p c t i", i=RUN),
            )

        def quantise_h():
            nc.vector.quantize_mx(
                out=h_codes[:].bitcast(FP8X4),
                scales=h_scales[:],
                in_=h_grouped[:].rearrange("p r t -> p (r t)"),
            )

        def multiply_tail(m):
            tokens = slice(P * m, P * (m + 1))
            for n in range(TAIL_BANKS):
                columns = slice(BANK * n, BANK * (n + 1))
                tail_logits[(m, n)] = bank(4 + n, "tail_logits")
                nc.tensor.matmul_mx(
                    out=tail_logits[(m, n)],
                    lhsT=h_codes[:, tokens].bitcast(FP8X4),
                    lhsT_scale=h_scales[:, tokens],
                    rhs=tail_codes[:, columns].bitcast(FP8X4),
                    rhs_scale=tail_scales[:, columns],
                    start=True,
                    stop=True,
                )

        def max_tail(m):
            for n in range(TAIL_BANKS):
                nc.vector.reduce_max(
                    out=tail_bank_max[m][:, n : n + 1], in_=tail_logits[(m, n)], axis=ALONG_ROW
                )
            nc.vector.tensor_reduce(
                out=tail_neg_max[m][:], in_=tail_bank_max[m][:], axis=ALONG_ROW, op=MAX, negate=True
            )

        def exp_tail(m):
            for n in range(TAIL_BANKS):
                nc.scalar.activation(
                    out=tail_exp[m][:, BANK * n : BANK * (n + 1)],
                    in_=tail_logits[(m, n)],
                    func=EXP,
                    bias=tail_neg_max[m][:],
                    accum_out=tail_bank_sum[m][:, n : n + 1],
                )

        def invert_tail_sum(m):
            nc.vector.reduce_sum(out=tail_sum[m][:], in_=tail_bank_sum[m][:], axis=ALONG_ROW)
            nc.vector.reciprocal(out=tail_inverse[m][:], in_=tail_sum[m][:])

        tail_stages = [round_h, regroup_h, quantise_h]
        for m in range(TOKEN_TILES):
            tail_stages.extend([lambda m=m: multiply_tail(m), lambda m=m: max_tail(m)])
            if m < TOKEN_TILES - 1:
                tail_stages.extend([lambda m=m: exp_tail(m), lambda m=m: invert_tail_sum(m)])

        HEAD_BANKS = HEAD // BANK
        head_acc = [
            [bank(HEAD_BANKS * m + n, "head_acc%d%d" % (m, n)) for n in range(HEAD_BANKS)]
            for m in range(TOKEN_TILES)
        ]

        def multiply_head(c, codes, scales):
            for m in range(TOKEN_TILES):
                tokens = slice(TOKENS * c + P * m, TOKENS * c + P * (m + 1))
                for n in range(HEAD_BANKS):
                    columns = slice(BANK * n, BANK * (n + 1))
                    nc.tensor.matmul_mx(
                        out=head_acc[m][n],
                        lhsT=x_codes[:, tokens].bitcast(FP8X4),
                        lhsT_scale=x_scales[:, tokens],
                        rhs=codes[:, columns].bitcast(FP8X4),
                        rhs_scale=scales[:, columns],
                        start=(c == 0),
                        stop=(c == PASSES - 1),
                    )

        for c in range(PASSES):
            raw = raw_pool.tile([P, CHUNK * PACK], BF16, name="raw")
            rows = raw[:].rearrange("p (t w) -> p t w", t=PACK)
            nc.sync.dma_start(
                out=rows,
                in_=head_weight[K_PASS * c : K_PASS * (c + 1), :].rearrange(
                    "(p t) w -> p t w", t=PACK
                ),
            )
            step(column_pieces(rows), None, None, multiply_head, c)
            if c < len(tail_stages):
                tail_stages[c]()
        for job in regrouped[-LAG:]:
            quantise_and_multiply(job)
        exp_tail(TOKEN_TILES - 1)
        invert_tail_sum(TOKEN_TILES - 1)

        head_exp = [keep.tile([P, HEAD], F32, name="head_exp%d" % m) for m in range(TOKEN_TILES)]
        head_bank_max = [
            keep.tile([P, HEAD_BANKS], F32, name="head_bank_max%d" % m) for m in range(TOKEN_TILES)
        ]
        head_neg_max = [keep.tile([P, 1], F32, name="head_neg_max%d" % m) for m in range(TOKEN_TILES)]
        head_bank_sum = [
            keep.tile([P, HEAD_BANKS], F32, name="head_bank_sum%d" % m) for m in range(TOKEN_TILES)
        ]
        head_sum = [keep.tile([P, 1], F32, name="head_sum%d" % m) for m in range(TOKEN_TILES)]
        head_inverse = [keep.tile([P, 1], F32, name="head_inverse%d" % m) for m in range(TOKEN_TILES)]
        tail_factor = [keep.tile([P, 1], F32, name="tail_factor%d" % m) for m in range(TOKEN_TILES)]

        for m in range(TOKEN_TILES):
            for n in range(HEAD_BANKS):
                nc.vector.reduce_max(
                    out=head_bank_max[m][:, n : n + 1], in_=head_acc[m][n], axis=ALONG_ROW
                )
            nc.vector.tensor_reduce(
                out=head_neg_max[m][:], in_=head_bank_max[m][:], axis=ALONG_ROW, op=MAX, negate=True
            )
        for m in range(TOKEN_TILES):
            for n in range(HEAD_BANKS):
                nc.scalar.activation(
                    out=head_exp[m][:, BANK * n : BANK * (n + 1)],
                    in_=head_acc[m][n],
                    func=EXP,
                    bias=head_neg_max[m][:],
                    accum_out=head_bank_sum[m][:, n : n + 1],
                )
        for m in range(TOKEN_TILES):
            nc.vector.reduce_sum(out=head_sum[m][:], in_=head_bank_sum[m][:], axis=ALONG_ROW)
            nc.vector.reciprocal(out=head_inverse[m][:], in_=head_sum[m][:])
            nc.vector.tensor_scalar(
                out=tail_factor[m][:],
                in0=head_exp[m][:, HEAD_TOKENS : HEAD_TOKENS + 1],
                scalar1=head_inverse[m][:],
                scalar2=tail_inverse[m][:],
                op0=MULT,
                op1=MULT,
            )
            nc.vector.tensor_scalar(
                out=cluster1[:, m : m + 1],
                in0=head_exp[m][:, HEAD_TOKENS + 1 : HEAD_TOKENS + 2],
                scalar1=head_inverse[m][:],
                scalar2=None,
                op0=MULT,
            )
            for first in range(0, TAIL, STORE_COLUMNS):
                columns = slice(first, first + STORE_COLUMNS)
                nc.vector.tensor_scalar(
                    out=tail_exp[m][:, columns],
                    in0=tail_exp[m][:, columns],
                    scalar1=tail_factor[m][:],
                    scalar2=None,
                    op0=MULT,
                )
                nc.sync.dma_start(
                    out=out_0[m, :, HEAD_TOKENS + first : HEAD_TOKENS + first + STORE_COLUMNS],
                    in_=tail_exp[m][:, columns],
                )
            nc.scalar.activation(
                out=head_exp[m][:, 0:HEAD_TOKENS],
                in_=head_exp[m][:, 0:HEAD_TOKENS],
                func=COPY,
                scale=head_inverse[m][:],
            )
            nc.sync.dma_start(out=out_0[m, :, 0:HEAD_TOKENS], in_=head_exp[m][:, 0:HEAD_TOKENS])

        cluster1_rows = bank(4, "cluster1_rows")
        nc.tensor.transpose(cluster1_rows[:, 0:P], cluster1[:], identity[:])
        cluster1_out = keep.tile([P, P], F32, name="cluster1_out")
        nc.scalar.copy(out=cluster1_out[:], in_=cluster1_rows[:, 0:P])
        nc.sync.dma_start(
            out=out_1.rearrange("n t o -> n (t o)"), in_=cluster1_out[0:TOKEN_TILES, :]
        )
